import numpy as np
import ml_dtypes


def mxq(x, axis, fmt="e4m3"):
    dtype, down = {"e4m3": (ml_dtypes.float8_e4m3fn, 7), "e5m2": (ml_dtypes.float8_e5m2, 14)}[fmt]
    v = np.moveaxis(np.asarray(x, np.float32).astype(ml_dtypes.bfloat16).astype(np.float64), axis, -1)
    blocks = v.reshape(v.shape[:-1] + (-1, 32))
    amax = np.abs(blocks).max(-1, keepdims=True)
    byte = np.maximum(np.where(amax > 0, np.frexp(amax)[1] - 1 + 127, 0) - down, 1)
    scale = np.exp2(byte - 127.0)
    codes = (blocks / scale).astype(np.float32).astype(dtype).astype(np.float64)
    return np.moveaxis((codes * scale).reshape(v.shape), -1, axis)


WIDE = False


def mx_kscale(k):
    if not WIDE:
        return np.ones(k)
    levels = np.array([10, -10, 5, -5, 0])
    a = np.random.permutation(np.resize(levels, k // 512 * 4)).reshape(k // 512, 4)
    idx = np.arange(k)
    return np.exp2(a[idx // 512, idx % 128 // 32])


BF16 = ml_dtypes.bfloat16


def bf(x):
    return np.asarray(x, np.float32).astype(BF16)


def f64(x):
    return np.asarray(x).astype(np.float64)


B, S, H, N, L = 2, 4096, 512, 256, 20
EPS = 1e-06
XS = np.sqrt(4.0 * EPS * L * H / N)


def setup_inputs():
    s = mx_kscale(H)
    return {"hidden_states": bf(np.random.standard_normal((B, S, H)) * XS * s),
            "conv_w": bf(np.random.standard_normal((L, N, H)) / np.sqrt(H) / s),
            "norm_w": bf(1.0 + 0.1 * np.random.standard_normal(N))}


def reference(hidden_states, conv_w, norm_w):
    x = f64(hidden_states)
    w_sum = f64(conv_w).sum(axis=0)
    out = (mxq(x, 2, "e4m3") @ mxq(w_sum, 1, "e4m3").T) / L
    sq = np.sum(out * out, axis=-1, keepdims=True)
    norm_x = np.sqrt(sq + EPS * H)
    x_normed = out / norm_x * np.sqrt(H)
    return x_normed * f64(norm_w)

@@ -1,0 +1,210 @@
+import math
+from contextlib import ExitStack
+
+import concourse.mybir as mybir
+from concourse.masks import make_identity
+
+F32 = mybir.dt.float32
+BF16 = mybir.dt.bfloat16
+U32 = mybir.dt.uint32
+U8 = mybir.dt.uint8
+FP8X4 = mybir.dt.float8_e4m3fn_x4
+ALU = mybir.AluOpType
+ACT = mybir.ActivationFunctionType
+
+P = 128
+TOKENS = 8192
+H = 512
+K = 256
+LAYERS = 20
+EPS = 1e-06
+TILES = TOKENS // P
+RT = 4
+ROUNDS = TILES // RT
+
+FLOPS = 2 * TOKENS * H * K
+
+W_CHUNKS = [(0, 1), (1, 2), (2, 4), (4, 6), (6, 7), (7, 8)]
+X_CHUNKS = [(0, 4), (4, 8), (8, 16), (16, 24), (24, 32), (32, 40), (40, 48), (48, 56), (56, 64)]
+VECTOR_COPY_ROUNDS = (1, 4, 7, 10, 13)
+
+
+def tile_conv2dlinalgrmsnorm_t_kernel(tc, hidden_states, conv_w, norm_w, out):
+    nc = tc.nc
+    xv = hidden_states.flatten_outer_dims().rearrange("(p t) h -> p (t h)", t=TILES)
+    ov = out.flatten_outer_dims().rearrange("(p t) k -> p (t k)", t=TILES)
+    wv = conv_w.flatten_outer_dims().rearrange("(i p g) h -> p i g h", i=5, p=P, g=8)
+
+    with ExitStack() as ctx:
+        keep = ctx.enter_context(tc.tile_pool(name="keep", bufs=1))
+        stage = ctx.enter_context(tc.tile_pool(name="stage", bufs=3))
+        psum = ctx.enter_context(tc.psum_pool(name="psum", bufs=4))
+        ctx.enter_context(tc.manual_schedule())
+
+        w5 = keep.tile([P, 5, 8, H], BF16)
+        x_sb = keep.tile([P, TILES * H], BF16)
+        out_sb = keep.tile([P, TILES * K], F32)
+        ident = keep.tile([P, P], F32)
+        sel_f = keep.tile([P, 32], F32)
+        sel = keep.tile([P, 32], BF16)
+        ones = keep.tile([P, P], BF16)
+        nwz = keep.tile([P, K], BF16)
+        nwp = keep.tile([P, K], F32)
+        epsb = keep.tile([P, 1], F32)
+        warm = keep.tile([P, 1], F32)
+        junk = keep.tile([P, K], BF16)
+        wg = keep.tile([P, 4 * K], BF16, align_bytes=64)
+        w_codes = keep.tile([P, K], U32, align_bytes=64)
+        w_scales = keep.tile([P, K], U8, align_bytes=64)
+
+        for g0, g1 in W_CHUNKS:
+            nc.sync.dma_start(out=w5[:, :, g0:g1, :], in_=wv[:, :, g0:g1, :])
+        for t0, t1 in X_CHUNKS:
+            nc.sync.dma_start(out=x_sb[:, t0 * H : t1 * H], in_=xv[:, t0 * H : t1 * H])
+
+        nc.vector.memset(epsb[:], EPS * H)
+        nc.vector.memset(nwz[:], 0.0)
+        nc.vector.memset(ones[:], 1.0)
+        nc.scalar.dma_start(out=nwz[0:1, :], in_=norm_w.unsqueeze(0))
+        nc.scalar.activation(out=warm[:], in_=epsb[:], func=ACT.Sqrt)
+        make_identity(nc, ident[:])
+        nc.vector.tensor_reduce(
+            out=sel_f[:],
+            in_=ident[:].rearrange("p (a n) -> p n a", a=4),
+            axis=mybir.AxisListType.X,
+            op=ALU.add,
+        )
+        nc.vector.tensor_copy(out=sel[:], in_=sel_f[:])
+        nw_ps = psum.tile([P, K], F32, tag="y")
+        nc.tensor.matmul(out=nw_ps[:], lhsT=ones[:], rhs=nwz[:], start=True, stop=True)
+        nc.vector.tensor_scalar_mul(out=nwp[:], in0=nw_ps[:], scalar1=math.sqrt(H) / LAYERS)
+
+        wg4 = wg[:].rearrange("p (j g t) -> p j g t", j=32, g=8, t=4)
+        for b in range(2):
+            wt = psum.tile([P, 4, 4, 32], F32, tag="xt")
+            for gl in range(4):
+                g = 4 * b + gl
+                for t in range(4):
+                    u, e = divmod(t, 2)
+                    for i in range(5):
+                        nc.tensor.matmul(
+                            out=wt[:, t, gl, :],
+                            lhsT=w5[:, i, g, 256 * u + e : 256 * u + 256 : 2],
+                            rhs=sel[:],
+                            start=(i == 0),
+                            stop=(i == 4),
+                        )
+            nc.vector.tensor_copy(
+                out=wg4[:, :, 4 * b : 4 * b + 4, :],
+                in_=wt[:].rearrange("p t g j -> p j g t"),
+            )
+        nc.vector.quantize_mx(out=w_codes[:].bitcast(FP8X4), scales=w_scales[:], in_=wg[:])
+
+        xw = x_sb[:].bitcast(F32)
+        xt_of = {}
+        grp_of = {}
+        code_of = {}
+        y_of = {}
+        stat_of = {}
+
+        def transposes(k):
+            banks = []
+            for b in range(2):
+                xt = psum.tile([P, 2, 2, P], F32, tag="xt")
+                for a in range(2):
+                    t = RT * k + 2 * b + a
+                    for u in range(2):
+                        c0 = 256 * t + P * u
+                        nc.tensor.transpose(xt[:, a, u, :], xw[:, c0 : c0 + P], ident[:])
+                banks.append(xt)
+            xt_of[k] = banks
+
+        def copy_out(k, b, on_vector):
+            if b == 0:
+                grp = stage.tile([P, RT * H], BF16, align_bytes=64, tag="grp")
+                grp_of[k] = grp
+            g32 = grp_of[k][:].bitcast(F32)
+            dst = g32[:, 512 * b : 512 * b + 512].rearrange("p (a r u) -> p a r u", a=2, r=P, u=2)
+            src = xt_of[k][b][:].rearrange("p a u r -> p a r u")
+            if on_vector:
+                nc.vector.tensor_copy(out=dst, in_=src)
+            else:
+                nc.scalar.copy(out=dst, in_=src)
+
+        def quantise(k):
+            xc = stage.tile([P, RT * P], U32, align_bytes=64, tag="xc")
+            xs = stage.tile([P, RT * P], U8, align_bytes=64, tag="xs")
+            nc.vector.quantize_mx(out=xc[:].bitcast(FP8X4), scales=xs[:], in_=grp_of[k][:])
+            code_of[k] = (xc, xs)
+
+        def passes(k):
+            xc, xs = code_of[k]
+            banks = []
+            for b in range(2):
+                y = psum.tile([P, 2, K], F32, tag="y")
+                for a in range(2):
+                    c0 = P * (2 * b + a)
+                    nc.tensor.matmul_mx(
+                        out=y[:, a, :],
+                        lhsT=xc[:, c0 : c0 + P].bitcast(FP8X4),
+                        lhsT_scale=xs[:, c0 : c0 + P],
+                        rhs=w_codes[:].bitcast(FP8X4),
+                        rhs_scale=w_scales[:],
+                        start=True,
+                        stop=True,
+                    )
+                banks.append(y)
+            y_of[k] = banks
+
+        def squares(k):
+            q = stage.tile([P, RT], F32, tag="q")
+            n = stage.tile([P, RT], F32, tag="n")
+            for j in range(RT):
+                nc.scalar.activation(
+                    out=junk[:],
+                    in_=y_of[k][j // 2][:, j % 2, :],
+                    func=ACT.Square,
+                    accum_out=q[:, j : j + 1],
+                )
+            nc.scalar.activation(
+                out=n[:], in_=q[:], func=ACT.Sqrt, bias=epsb[:], scale=1.0 / (LAYERS * LAYERS)
+            )
+            stat_of[k] = n
+
+        def reciprocal(k):
+            r = stage.tile([P, RT], F32, tag="r")
+            nc.vector.reciprocal(out=r[:], in_=stat_of[k][:])
+            stat_of[k] = r
+
+        def final(k):
+            r = stat_of[k]
+            for j in range(RT):
+                t = RT * k + j
+                nc.vector.scalar_tensor_tensor(
+                    out=out_sb[:, t * K : (t + 1) * K],
+                    in0=y_of[k][j // 2][:, j % 2, :],
+                    scalar=r[:, j : j + 1],
+                    in1=nwp[:],
+                    op0=ALU.mult,
+                    op1=ALU.mult,
+                )
+            c0 = RT * k * K
+            nc.sync.dma_start(out=ov[:, c0 : c0 + RT * K], in_=out_sb[:, c0 : c0 + RT * K])
+
+        for k in range(-2, ROUNDS + 1):
+            if 0 <= k < ROUNDS:
+                passes(k)
+            if 0 <= k + 2 < ROUNDS:
+                transposes(k + 2)
+            if 0 <= k + 1 < ROUNDS:
+                copy_out(k + 1, 0, False)
+            if 0 <= k - 1 < ROUNDS:
+                reciprocal(k - 1)
+            if 0 <= k + 1 < ROUNDS:
+                copy_out(k + 1, 1, (k + 1) in VECTOR_COPY_ROUNDS)
+            if 0 <= k < ROUNDS:
+                squares(k)
+            if 0 <= k - 1 < ROUNDS:
+                final(k - 1)
+            if 0 <= k + 1 < ROUNDS:
+                quantise(k + 1)

@@ -21,12 +21,14 @@ EPS = 1e-06
 TILES = TOKENS // P
 RT = 4
 ROUNDS = TILES // RT
+LEAD = 2
+DUMMIES = 0
 
 FLOPS = 2 * TOKENS * H * K
 
 W_CHUNKS = [(0, 1), (1, 2), (2, 4), (4, 6), (6, 7), (7, 8)]
-X_CHUNKS = [(0, 4), (4, 8), (8, 16), (16, 24), (24, 32), (32, 40), (40, 48), (48, 56), (56, 64)]
-VECTOR_COPY_ROUNDS = (1, 4, 7, 10, 13)
+X_CHUNKS = [(0, 4), (4, 8), (8, 12), (12, 16), (16, 24), (24, 32), (32, 40), (40, 48), (48, 56), (56, 64)]
+VECTOR_COPY_ROUNDS = (4, 6, 8, 10, 12, 14)
 
 
 def tile_conv2dlinalgrmsnorm_t_kernel(tc, hidden_states, conv_w, norm_w, out):
@@ -38,6 +40,7 @@ def tile_conv2dlinalgrmsnorm_t_kernel(tc, hidden_states, conv_w, norm_w, out):
     with ExitStack() as ctx:
         keep = ctx.enter_context(tc.tile_pool(name="keep", bufs=1))
         stage = ctx.enter_context(tc.tile_pool(name="stage", bufs=3))
+        codes = ctx.enter_context(tc.tile_pool(name="codes", bufs=LEAD + 3))
         psum = ctx.enter_context(tc.psum_pool(name="psum", bufs=4))
         ctx.enter_context(tc.manual_schedule())
 
@@ -45,6 +48,7 @@ def tile_conv2dlinalgrmsnorm_t_kernel(tc, hidden_states, conv_w, norm_w, out):
         x_sb = keep.tile([P, TILES * H], BF16)
         out_sb = keep.tile([P, TILES * K], F32)
         ident = keep.tile([P, P], F32)
+        ident_b = keep.tile([P, P], BF16)
         sel_f = keep.tile([P, 32], F32)
         sel = keep.tile([P, 32], BF16)
         ones = keep.tile([P, P], BF16)
@@ -53,19 +57,23 @@ def tile_conv2dlinalgrmsnorm_t_kernel(tc, hidden_states, conv_w, norm_w, out):
         epsb = keep.tile([P, 1], F32)
         warm = keep.tile([P, 1], F32)
         junk = keep.tile([P, K], BF16)
+        ws1 = keep.tile([P, 2, 4, P], BF16)
+        ws3 = keep.tile([P, 2, H], BF16)
         wg = keep.tile([P, 4 * K], BF16, align_bytes=64)
         w_codes = keep.tile([P, K], U32, align_bytes=64)
         w_scales = keep.tile([P, K], U8, align_bytes=64)
 
+        nc.vector.memset(nwz[:], 0.0)
+        nc.vector.memset(epsb[:], EPS * H)
+        nc.vector.memset(ones[:], 1.0)
+        first = True
         for g0, g1 in W_CHUNKS:
             nc.sync.dma_start(out=w5[:, :, g0:g1, :], in_=wv[:, :, g0:g1, :])
+            if first:
+                nc.sync.dma_start(out=nwz[0:1, :], in_=norm_w.unsqueeze(0))
+                first = False
         for t0, t1 in X_CHUNKS:
             nc.sync.dma_start(out=x_sb[:, t0 * H : t1 * H], in_=xv[:, t0 * H : t1 * H])
-
-        nc.vector.memset(epsb[:], EPS * H)
-        nc.vector.memset(nwz[:], 0.0)
-        nc.vector.memset(ones[:], 1.0)
-        nc.scalar.dma_start(out=nwz[0:1, :], in_=norm_w.unsqueeze(0))
         nc.scalar.activation(out=warm[:], in_=epsb[:], func=ACT.Sqrt)
         make_identity(nc, ident[:])
         nc.vector.tensor_reduce(
@@ -75,30 +83,49 @@ def tile_conv2dlinalgrmsnorm_t_kernel(tc, hidden_states, conv_w, norm_w, out):
             op=ALU.add,
         )
         nc.vector.tensor_copy(out=sel[:], in_=sel_f[:])
-        nw_ps = psum.tile([P, K], F32, tag="y")
-        nc.tensor.matmul(out=nw_ps[:], lhsT=ones[:], rhs=nwz[:], start=True, stop=True)
-        nc.vector.tensor_scalar_mul(out=nwp[:], in0=nw_ps[:], scalar1=math.sqrt(H) / LAYERS)
+        nc.vector.tensor_copy(out=ident_b[:], in_=ident[:])
 
+        wt0 = psum.tile([P, 4, P], F32, tag="y")
+        wt1 = psum.tile([P, 4, P], F32, tag="y")
+        wt = [wt0, wt1]
+        s2 = psum.tile([P, 2, H], BF16, tag="y")
+        s4 = psum.tile([P, 4, 2, P], BF16, tag="y")
         wg4 = wg[:].rearrange("p (j g t) -> p j g t", j=32, g=8, t=4)
-        for b in range(2):
-            wt = psum.tile([P, 4, 4, 32], F32, tag="xt")
-            for gl in range(4):
-                g = 4 * b + gl
-                for t in range(4):
-                    u, e = divmod(t, 2)
-                    for i in range(5):
-                        nc.tensor.matmul(
-                            out=wt[:, t, gl, :],
-                            lhsT=w5[:, i, g, 256 * u + e : 256 * u + 256 : 2],
-                            rhs=sel[:],
-                            start=(i == 0),
-                            stop=(i == 4),
-                        )
+
+        def w_sum(g):
+            b, gl = divmod(g, 4)
+            for t in range(4):
+                for i in range(5):
+                    nc.tensor.matmul(
+                        out=wt[b][:, t, 32 * gl : 32 * gl + 32],
+                        lhsT=w5[:, i, g, P * t : P * t + P],
+                        rhs=sel[:],
+                        start=(i == 0),
+                        stop=(i == 4),
+                    )
+
+        def w_round(b):
+            nc.vector.tensor_copy(out=ws1[:, b, :, :], in_=wt[b][:])
+
+        def w_back(b):
+            for t in range(4):
+                nc.tensor.transpose(s2[:, b, P * t : P * t + P], ws1[:, b, t, :], ident_b[:])
+
+        def w_back_copy(b):
+            nc.scalar.copy(out=ws3[:, b, :], in_=s2[:, b, :])
+
+        def w_forth(b):
+            for t in range(4):
+                u, e = divmod(t, 2)
+                nc.tensor.transpose(
+                    s4[:, t, b, :], ws3[:, b, 256 * u + e : 256 * u + 256 : 2], ident_b[:]
+                )
+
+        def w_forth_copy(b):
             nc.vector.tensor_copy(
                 out=wg4[:, :, 4 * b : 4 * b + 4, :],
-                in_=wt[:].rearrange("p t g j -> p j g t"),
+                in_=s4[:, :, b, :].rearrange("p t (g j) -> p j g t", g=4, j=32),
             )
-        nc.vector.quantize_mx(out=w_codes[:].bitcast(FP8X4), scales=w_scales[:], in_=wg[:])
 
         xw = x_sb[:].bitcast(F32)
         xt_of = {}
@@ -132,8 +159,8 @@ def tile_conv2dlinalgrmsnorm_t_kernel(tc, hidden_states, conv_w, norm_w, out):
                 nc.scalar.copy(out=dst, in_=src)
 
         def quantise(k):
-            xc = stage.tile([P, RT * P], U32, align_bytes=64, tag="xc")
-            xs = stage.tile([P, RT * P], U8, align_bytes=64, tag="xs")
+            xc = codes.tile([P, RT * P], U32, align_bytes=64, tag="xc")
+            xs = codes.tile([P, RT * P], U8, align_bytes=64, tag="xs")
             nc.vector.quantize_mx(out=xc[:].bitcast(FP8X4), scales=xs[:], in_=grp_of[k][:])
             code_of[k] = (xc, xs)
 
@@ -142,6 +169,16 @@ def tile_conv2dlinalgrmsnorm_t_kernel(tc, hidden_states, conv_w, norm_w, out):
             banks = []
             for b in range(2):
                 y = psum.tile([P, 2, K], F32, tag="y")
+                if b < DUMMIES:
+                    nc.tensor.matmul_mx(
+                        out=y[:].rearrange("p a k -> p (a k)"),
+                        lhsT=xc[:, 0:P].bitcast(FP8X4),
+                        lhsT_scale=xs[:, 0:P],
+                        rhs=xc[:].bitcast(FP8X4),
+                        rhs_scale=xs[:],
+                        start=True,
+                        stop=True,
+                    )
                 for a in range(2):
                     c0 = P * (2 * b + a)
                     nc.tensor.matmul_mx(
@@ -191,20 +228,58 @@ def tile_conv2dlinalgrmsnorm_t_kernel(tc, hidden_states, conv_w, norm_w, out):
             c0 = RT * k * K
             nc.sync.dma_start(out=ov[:, c0 : c0 + RT * K], in_=out_sb[:, c0 : c0 + RT * K])
 
-        for k in range(-2, ROUNDS + 1):
-            if 0 <= k < ROUNDS:
+        w_sum(0)
+        nw_ps = psum.tile([P, K], F32, tag="xt")
+        nc.tensor.matmul(out=nw_ps[:], lhsT=ones[:], rhs=nwz[:], start=True, stop=True)
+        nc.vector.tensor_scalar_mul(out=nwp[:], in0=nw_ps[:], scalar1=math.sqrt(H) / LAYERS)
+        w_sum(1)
+        w_sum(2)
+        w_sum(3)
+        w_round(0)
+        w_sum(4)
+        w_back(0)
+        w_back_copy(0)
+        w_sum(5)
+        w_forth(0)
+        w_forth_copy(0)
+        w_sum(6)
+        w_sum(7)
+        w_round(1)
+        transposes(0)
+        w_back(1)
+        copy_out(0, 0, True)
+        copy_out(0, 1, True)
+        w_back_copy(1)
+        transposes(1)
+        w_forth(1)
+        copy_out(1, 0, False)
+        copy_out(1, 1, False)
+        w_forth_copy(1)
+        quantise(0)
+        nc.vector.quantize_mx(out=w_codes[:].bitcast(FP8X4), scales=w_scales[:], in_=wg[:])
+        for r in range(2, LEAD + 1):
+            transposes(r)
+            copy_out(r, 0, False)
+            copy_out(r, 1, False)
+            quantise(r - 1)
+        transposes(LEAD + 1)
+        quantise(LEAD)
+
+        for k in range(ROUNDS + 1):
+            a = k + LEAD + 1
+            if k < ROUNDS:
                 passes(k)
-            if 0 <= k + 2 < ROUNDS:
-                transposes(k + 2)
-            if 0 <= k + 1 < ROUNDS:
-                copy_out(k + 1, 0, False)
-            if 0 <= k - 1 < ROUNDS:
+            if a + 1 < ROUNDS:
+                transposes(a + 1)
+            if a < ROUNDS:
+                copy_out(a, 0, False)
+            if k >= 1:
                 reciprocal(k - 1)
-            if 0 <= k + 1 < ROUNDS:
-                copy_out(k + 1, 1, (k + 1) in VECTOR_COPY_ROUNDS)
-            if 0 <= k < ROUNDS:
+            if a < ROUNDS:
+                copy_out(a, 1, a in VECTOR_COPY_ROUNDS)
+            if k < ROUNDS:
                 squares(k)
-            if 0 <= k - 1 < ROUNDS:
+            if k >= 1:
                 final(k - 1)
-            if 0 <= k + 1 < ROUNDS:
-                quantise(k + 1)
+            if a < ROUNDS:
+                quantise(a)

@@ -41,7 +41,8 @@ def tile_conv2dlinalgrmsnorm_t_kernel(tc, hidden_states, conv_w, norm_w, out):
         keep = ctx.enter_context(tc.tile_pool(name="keep", bufs=1))
         stage = ctx.enter_context(tc.tile_pool(name="stage", bufs=3))
         codes = ctx.enter_context(tc.tile_pool(name="codes", bufs=LEAD + 3))
-        psum = ctx.enter_context(tc.psum_pool(name="psum", bufs=4))
+        psum_x = ctx.enter_context(tc.psum_pool(name="psum_x", bufs=2))
+        psum_y = ctx.enter_context(tc.psum_pool(name="psum_y", bufs=6))
         ctx.enter_context(tc.manual_schedule())
 
         w5 = keep.tile([P, 5, 8, H], BF16)
@@ -85,11 +86,11 @@ def tile_conv2dlinalgrmsnorm_t_kernel(tc, hidden_states, conv_w, norm_w, out):
         nc.vector.tensor_copy(out=sel[:], in_=sel_f[:])
         nc.vector.tensor_copy(out=ident_b[:], in_=ident[:])
 
-        wt0 = psum.tile([P, 4, P], F32, tag="y")
-        wt1 = psum.tile([P, 4, P], F32, tag="y")
+        wt0 = psum_y.tile([P, 4, P], F32, tag="y")
+        wt1 = psum_y.tile([P, 4, P], F32, tag="y")
         wt = [wt0, wt1]
-        s2 = psum.tile([P, 2, H], BF16, tag="y")
-        s4 = psum.tile([P, 4, 2, P], BF16, tag="y")
+        s2 = psum_y.tile([P, 2, H], BF16, tag="y")
+        s4 = psum_y.tile([P, 4, 2, P], BF16, tag="y")
         wg4 = wg[:].rearrange("p (j g t) -> p j g t", j=32, g=8, t=4)
 
         def w_sum(g):
@@ -137,7 +138,7 @@ def tile_conv2dlinalgrmsnorm_t_kernel(tc, hidden_states, conv_w, norm_w, out):
         def transposes(k):
             banks = []
             for b in range(2):
-                xt = psum.tile([P, 2, 2, P], F32, tag="xt")
+                xt = psum_x.tile([P, 2, 2, P], F32, tag="xt")
                 for a in range(2):
                     t = RT * k + 2 * b + a
                     for u in range(2):
@@ -168,7 +169,7 @@ def tile_conv2dlinalgrmsnorm_t_kernel(tc, hidden_states, conv_w, norm_w, out):
             xc, xs = code_of[k]
             banks = []
             for b in range(2):
-                y = psum.tile([P, 2, K], F32, tag="y")
+                y = psum_y.tile([P, 2, K], F32, tag="y")
                 if b < DUMMIES:
                     nc.tensor.matmul_mx(
                         out=y[:].rearrange("p a k -> p (a k)"),
@@ -229,7 +230,7 @@ def tile_conv2dlinalgrmsnorm_t_kernel(tc, hidden_states, conv_w, norm_w, out):
             nc.sync.dma_start(out=ov[:, c0 : c0 + RT * K], in_=out_sb[:, c0 : c0 + RT * K])
 
         w_sum(0)
-        nw_ps = psum.tile([P, K], F32, tag="xt")
+        nw_ps = psum_x.tile([P, K], F32, tag="xt")
         nc.tensor.matmul(out=nw_ps[:], lhsT=ones[:], rhs=nwz[:], start=True, stop=True)
         nc.vector.tensor_scalar_mul(out=nwp[:], in0=nw_ps[:], scalar1=math.sqrt(H) / LAYERS)
         w_sum(1)
@@ -265,18 +266,19 @@ def tile_conv2dlinalgrmsnorm_t_kernel(tc, hidden_states, conv_w, norm_w, out):
         transposes(LEAD + 1)
         quantise(LEAD)
 
+        passes(0)
         for k in range(ROUNDS + 1):
             a = k + LEAD + 1
-            if k < ROUNDS:
-                passes(k)
-            if a + 1 < ROUNDS:
-                transposes(a + 1)
+            if k + 1 < ROUNDS:
+                passes(k + 1)
             if a < ROUNDS:
                 copy_out(a, 0, False)
             if k >= 1:
                 reciprocal(k - 1)
             if a < ROUNDS:
                 copy_out(a, 1, a in VECTOR_COPY_ROUNDS)
+            if a + 1 < ROUNDS:
+                transposes(a + 1)
             if k < ROUNDS:
                 squares(k)
             if k >= 1:

@@ -22,7 +22,7 @@ TILES = TOKENS // P
 RT = 4
 ROUNDS = TILES // RT
 LEAD = 2
-DUMMIES = 0
+DUMMIES = 2
 
 FLOPS = 2 * TOKENS * H * K
 
@@ -41,8 +41,7 @@ def tile_conv2dlinalgrmsnorm_t_kernel(tc, hidden_states, conv_w, norm_w, out):
         keep = ctx.enter_context(tc.tile_pool(name="keep", bufs=1))
         stage = ctx.enter_context(tc.tile_pool(name="stage", bufs=3))
         codes = ctx.enter_context(tc.tile_pool(name="codes", bufs=LEAD + 3))
-        psum_x = ctx.enter_context(tc.psum_pool(name="psum_x", bufs=2))
-        psum_y = ctx.enter_context(tc.psum_pool(name="psum_y", bufs=6))
+        psum = ctx.enter_context(tc.psum_pool(name="psum", bufs=4))
         ctx.enter_context(tc.manual_schedule())
 
         w5 = keep.tile([P, 5, 8, H], BF16)
@@ -86,11 +85,11 @@ def tile_conv2dlinalgrmsnorm_t_kernel(tc, hidden_states, conv_w, norm_w, out):
         nc.vector.tensor_copy(out=sel[:], in_=sel_f[:])
         nc.vector.tensor_copy(out=ident_b[:], in_=ident[:])
 
-        wt0 = psum_y.tile([P, 4, P], F32, tag="y")
-        wt1 = psum_y.tile([P, 4, P], F32, tag="y")
+        wt0 = psum.tile([P, 4, P], F32, tag="y")
+        wt1 = psum.tile([P, 4, P], F32, tag="y")
         wt = [wt0, wt1]
-        s2 = psum_y.tile([P, 2, H], BF16, tag="y")
-        s4 = psum_y.tile([P, 4, 2, P], BF16, tag="y")
+        s2 = psum.tile([P, 2, H], BF16, tag="y")
+        s4 = psum.tile([P, 4, 2, P], BF16, tag="y")
         wg4 = wg[:].rearrange("p (j g t) -> p j g t", j=32, g=8, t=4)
 
         def w_sum(g):
@@ -138,7 +137,7 @@ def tile_conv2dlinalgrmsnorm_t_kernel(tc, hidden_states, conv_w, norm_w, out):
         def transposes(k):
             banks = []
             for b in range(2):
-                xt = psum_x.tile([P, 2, 2, P], F32, tag="xt")
+                xt = psum.tile([P, 2, 2, P], F32, tag="xt")
                 for a in range(2):
                     t = RT * k + 2 * b + a
                     for u in range(2):
@@ -169,7 +168,7 @@ def tile_conv2dlinalgrmsnorm_t_kernel(tc, hidden_states, conv_w, norm_w, out):
             xc, xs = code_of[k]
             banks = []
             for b in range(2):
-                y = psum_y.tile([P, 2, K], F32, tag="y")
+                y = psum.tile([P, 2, K], F32, tag="y")
                 if b < DUMMIES:
                     nc.tensor.matmul_mx(
                         out=y[:].rearrange("p a k -> p (a k)"),
@@ -230,7 +229,7 @@ def tile_conv2dlinalgrmsnorm_t_kernel(tc, hidden_states, conv_w, norm_w, out):
             nc.sync.dma_start(out=ov[:, c0 : c0 + RT * K], in_=out_sb[:, c0 : c0 + RT * K])
 
         w_sum(0)
-        nw_ps = psum_x.tile([P, K], F32, tag="xt")
+        nw_ps = psum.tile([P, K], F32, tag="xt")
         nc.tensor.matmul(out=nw_ps[:], lhsT=ones[:], rhs=nwz[:], start=True, stop=True)
         nc.vector.tensor_scalar_mul(out=nwp[:], in0=nw_ps[:], scalar1=math.sqrt(H) / LAYERS)
         w_sum(1)
@@ -266,19 +265,18 @@ def tile_conv2dlinalgrmsnorm_t_kernel(tc, hidden_states, conv_w, norm_w, out):
         transposes(LEAD + 1)
         quantise(LEAD)
 
-        passes(0)
         for k in range(ROUNDS + 1):
             a = k + LEAD + 1
-            if k + 1 < ROUNDS:
-                passes(k + 1)
+            if k < ROUNDS:
+                passes(k)
+            if a + 1 < ROUNDS:
+                transposes(a + 1)
             if a < ROUNDS:
                 copy_out(a, 0, False)
             if k >= 1:
                 reciprocal(k - 1)
             if a < ROUNDS:
                 copy_out(a, 1, a in VECTOR_COPY_ROUNDS)
-            if a + 1 < ROUNDS:
-                transposes(a + 1)
             if k < ROUNDS:
                 squares(k)
             if k >= 1:

@@ -22,13 +22,13 @@ TILES = TOKENS // P
 RT = 4
 ROUNDS = TILES // RT
 LEAD = 2
-DUMMIES = 2
+DUMMIES = 0
 
 FLOPS = 2 * TOKENS * H * K
 
 W_CHUNKS = [(0, 1), (1, 2), (2, 4), (4, 6), (6, 7), (7, 8)]
 X_CHUNKS = [(0, 4), (4, 8), (8, 12), (12, 16), (16, 24), (24, 32), (32, 40), (40, 48), (48, 56), (56, 64)]
-VECTOR_COPY_ROUNDS = (4, 6, 8, 10, 12, 14)
+VECTOR_COPY_ROUNDS = (3, 4, 5, 6, 7, 8, 9, 10, 11, 12, 13, 14, 15)
 
 
 def tile_conv2dlinalgrmsnorm_t_kernel(tc, hidden_states, conv_w, norm_w, out):

@@ -28,7 +28,6 @@ FLOPS = 2 * TOKENS * H * K
 
 W_CHUNKS = [(0, 1), (1, 2), (2, 4), (4, 6), (6, 7), (7, 8)]
 X_CHUNKS = [(0, 4), (4, 8), (8, 12), (12, 16), (16, 24), (24, 32), (32, 40), (40, 48), (48, 56), (56, 64)]
-VECTOR_COPY_ROUNDS = (3, 4, 5, 6, 7, 8, 9, 10, 11, 12, 13, 14, 15)
 
 
 def tile_conv2dlinalgrmsnorm_t_kernel(tc, hidden_states, conv_w, norm_w, out):
@@ -41,7 +40,8 @@ def tile_conv2dlinalgrmsnorm_t_kernel(tc, hidden_states, conv_w, norm_w, out):
         keep = ctx.enter_context(tc.tile_pool(name="keep", bufs=1))
         stage = ctx.enter_context(tc.tile_pool(name="stage", bufs=3))
         codes = ctx.enter_context(tc.tile_pool(name="codes", bufs=LEAD + 3))
-        psum = ctx.enter_context(tc.psum_pool(name="psum", bufs=4))
+        psum_x = ctx.enter_context(tc.psum_pool(name="psum_x", bufs=3))
+        psum_y = ctx.enter_context(tc.psum_pool(name="psum_y", bufs=5))
         ctx.enter_context(tc.manual_schedule())
 
         w5 = keep.tile([P, 5, 8, H], BF16)
@@ -54,8 +54,7 @@ def tile_conv2dlinalgrmsnorm_t_kernel(tc, hidden_states, conv_w, norm_w, out):
         ones = keep.tile([P, P], BF16)
         nwz = keep.tile([P, K], BF16)
         nwp = keep.tile([P, K], F32)
-        epsb = keep.tile([P, 1], F32)
-        warm = keep.tile([P, 1], F32)
+        mhalf = keep.tile([P, RT], F32)
         junk = keep.tile([P, K], BF16)
         ws1 = keep.tile([P, 2, 4, P], BF16)
         ws3 = keep.tile([P, 2, H], BF16)
@@ -64,7 +63,7 @@ def tile_conv2dlinalgrmsnorm_t_kernel(tc, hidden_states, conv_w, norm_w, out):
         w_scales = keep.tile([P, K], U8, align_bytes=64)
 
         nc.vector.memset(nwz[:], 0.0)
-        nc.vector.memset(epsb[:], EPS * H)
+        nc.vector.memset(mhalf[:], -0.5)
         nc.vector.memset(ones[:], 1.0)
         first = True
         for g0, g1 in W_CHUNKS:
@@ -74,7 +73,6 @@ def tile_conv2dlinalgrmsnorm_t_kernel(tc, hidden_states, conv_w, norm_w, out):
                 first = False
         for t0, t1 in X_CHUNKS:
             nc.sync.dma_start(out=x_sb[:, t0 * H : t1 * H], in_=xv[:, t0 * H : t1 * H])
-        nc.scalar.activation(out=warm[:], in_=epsb[:], func=ACT.Sqrt)
         make_identity(nc, ident[:])
         nc.vector.tensor_reduce(
             out=sel_f[:],
@@ -85,11 +83,11 @@ def tile_conv2dlinalgrmsnorm_t_kernel(tc, hidden_states, conv_w, norm_w, out):
         nc.vector.tensor_copy(out=sel[:], in_=sel_f[:])
         nc.vector.tensor_copy(out=ident_b[:], in_=ident[:])
 
-        wt0 = psum.tile([P, 4, P], F32, tag="y")
-        wt1 = psum.tile([P, 4, P], F32, tag="y")
+        wt0 = psum_y.tile([P, 4, P], F32, tag="y")
+        wt1 = psum_y.tile([P, 4, P], F32, tag="y")
         wt = [wt0, wt1]
-        s2 = psum.tile([P, 2, H], BF16, tag="y")
-        s4 = psum.tile([P, 4, 2, P], BF16, tag="y")
+        s2 = psum_y.tile([P, 2, H], BF16, tag="y")
+        s4 = psum_y.tile([P, 4, 2, P], BF16, tag="y")
         wg4 = wg[:].rearrange("p (j g t) -> p j g t", j=32, g=8, t=4)
 
         def w_sum(g):
@@ -137,7 +135,7 @@ def tile_conv2dlinalgrmsnorm_t_kernel(tc, hidden_states, conv_w, norm_w, out):
         def transposes(k):
             banks = []
             for b in range(2):
-                xt = psum.tile([P, 2, 2, P], F32, tag="xt")
+                xt = psum_x.tile([P, 2, 2, P], F32, tag="xt")
                 for a in range(2):
                     t = RT * k + 2 * b + a
                     for u in range(2):
@@ -168,7 +166,7 @@ def tile_conv2dlinalgrmsnorm_t_kernel(tc, hidden_states, conv_w, norm_w, out):
             xc, xs = code_of[k]
             banks = []
             for b in range(2):
-                y = psum.tile([P, 2, K], F32, tag="y")
+                y = psum_y.tile([P, 2, K], F32, tag="y")
                 if b < DUMMIES:
                     nc.tensor.matmul_mx(
                         out=y[:].rearrange("p a k -> p (a k)"),
@@ -195,7 +193,6 @@ def tile_conv2dlinalgrmsnorm_t_kernel(tc, hidden_states, conv_w, norm_w, out):
 
         def squares(k):
             q = stage.tile([P, RT], F32, tag="q")
-            n = stage.tile([P, RT], F32, tag="n")
             for j in range(RT):
                 nc.scalar.activation(
                     out=junk[:],
@@ -203,14 +200,20 @@ def tile_conv2dlinalgrmsnorm_t_kernel(tc, hidden_states, conv_w, norm_w, out):
                     func=ACT.Square,
                     accum_out=q[:, j : j + 1],
                 )
-            nc.scalar.activation(
-                out=n[:], in_=q[:], func=ACT.Sqrt, bias=epsb[:], scale=1.0 / (LAYERS * LAYERS)
-            )
-            stat_of[k] = n
+            stat_of[k] = q
 
         def reciprocal(k):
+            n = stage.tile([P, RT], F32, tag="n")
             r = stage.tile([P, RT], F32, tag="r")
-            nc.vector.reciprocal(out=r[:], in_=stat_of[k][:])
+            nc.gpsimd.tensor_scalar(
+                out=n[:],
+                in0=stat_of[k][:],
+                scalar1=1.0 / (LAYERS * LAYERS),
+                scalar2=EPS * H,
+                op0=ALU.mult,
+                op1=ALU.add,
+            )
+            nc.gpsimd.tensor_tensor(out=r[:], in0=n[:], in1=mhalf[:], op=ALU.pow)
             stat_of[k] = r
 
         def final(k):
@@ -229,7 +232,7 @@ def tile_conv2dlinalgrmsnorm_t_kernel(tc, hidden_states, conv_w, norm_w, out):
             nc.sync.dma_start(out=ov[:, c0 : c0 + RT * K], in_=out_sb[:, c0 : c0 + RT * K])
 
         w_sum(0)
-        nw_ps = psum.tile([P, K], F32, tag="xt")
+        nw_ps = psum_x.tile([P, K], F32, tag="xt")
         nc.tensor.matmul(out=nw_ps[:], lhsT=ones[:], rhs=nwz[:], start=True, stop=True)
         nc.vector.tensor_scalar_mul(out=nwp[:], in0=nw_ps[:], scalar1=math.sqrt(H) / LAYERS)
         w_sum(1)
@@ -263,23 +266,22 @@ def tile_conv2dlinalgrmsnorm_t_kernel(tc, hidden_states, conv_w, norm_w, out):
             copy_out(r, 1, False)
             quantise(r - 1)
         transposes(LEAD + 1)
-        quantise(LEAD)
+        passes(0)
 
         for k in range(ROUNDS + 1):
             a = k + LEAD + 1
-            if k < ROUNDS:
-                passes(k)
-            if a + 1 < ROUNDS:
-                transposes(a + 1)
             if a < ROUNDS:
                 copy_out(a, 0, False)
+                copy_out(a, 1, a % 4 != 0)
+            if a + 1 < ROUNDS:
+                transposes(a + 1)
+            if a - 1 < ROUNDS:
+                quantise(a - 1)
             if k >= 1:
                 reciprocal(k - 1)
-            if a < ROUNDS:
-                copy_out(a, 1, a in VECTOR_COPY_ROUNDS)
             if k < ROUNDS:
                 squares(k)
             if k >= 1:
                 final(k - 1)
-            if a < ROUNDS:
-                quantise(a)
+            if k + 1 < ROUNDS:
+                passes(k + 1)

@@ -21,8 +21,7 @@ EPS = 1e-06
 TILES = TOKENS // P
 RT = 4
 ROUNDS = TILES // RT
-LEAD = 2
-DUMMIES = 0
+DUMMIES = 2
 
 FLOPS = 2 * TOKENS * H * K
 
@@ -39,7 +38,7 @@ def tile_conv2dlinalgrmsnorm_t_kernel(tc, hidden_states, conv_w, norm_w, out):
     with ExitStack() as ctx:
         keep = ctx.enter_context(tc.tile_pool(name="keep", bufs=1))
         stage = ctx.enter_context(tc.tile_pool(name="stage", bufs=3))
-        codes = ctx.enter_context(tc.tile_pool(name="codes", bufs=LEAD + 3))
+        codes = ctx.enter_context(tc.tile_pool(name="codes", bufs=3))
         psum_x = ctx.enter_context(tc.psum_pool(name="psum_x", bufs=3))
         psum_y = ctx.enter_context(tc.psum_pool(name="psum_y", bufs=5))
         ctx.enter_context(tc.manual_schedule())
@@ -54,7 +53,8 @@ def tile_conv2dlinalgrmsnorm_t_kernel(tc, hidden_states, conv_w, norm_w, out):
         ones = keep.tile([P, P], BF16)
         nwz = keep.tile([P, K], BF16)
         nwp = keep.tile([P, K], F32)
-        mhalf = keep.tile([P, RT], F32)
+        epsb = keep.tile([P, 1], F32)
+        warm = keep.tile([P, 1], F32)
         junk = keep.tile([P, K], BF16)
         ws1 = keep.tile([P, 2, 4, P], BF16)
         ws3 = keep.tile([P, 2, H], BF16)
@@ -63,7 +63,7 @@ def tile_conv2dlinalgrmsnorm_t_kernel(tc, hidden_states, conv_w, norm_w, out):
         w_scales = keep.tile([P, K], U8, align_bytes=64)
 
         nc.vector.memset(nwz[:], 0.0)
-        nc.vector.memset(mhalf[:], -0.5)
+        nc.vector.memset(epsb[:], EPS * H)
         nc.vector.memset(ones[:], 1.0)
         first = True
         for g0, g1 in W_CHUNKS:
@@ -73,6 +73,7 @@ def tile_conv2dlinalgrmsnorm_t_kernel(tc, hidden_states, conv_w, norm_w, out):
                 first = False
         for t0, t1 in X_CHUNKS:
             nc.sync.dma_start(out=x_sb[:, t0 * H : t1 * H], in_=xv[:, t0 * H : t1 * H])
+        nc.scalar.activation(out=warm[:], in_=epsb[:], func=ACT.Sqrt)
         make_identity(nc, ident[:])
         nc.vector.tensor_reduce(
             out=sel_f[:],
@@ -120,10 +121,12 @@ def tile_conv2dlinalgrmsnorm_t_kernel(tc, hidden_states, conv_w, norm_w, out):
                 )
 
         def w_forth_copy(b):
-            nc.vector.tensor_copy(
-                out=wg4[:, :, 4 * b : 4 * b + 4, :],
-                in_=s4[:, :, b, :].rearrange("p t (g j) -> p j g t", g=4, j=32),
-            )
+            dst = wg4[:, :, 4 * b : 4 * b + 4, :]
+            src = s4[:, :, b, :].rearrange("p t (g j) -> p j g t", g=4, j=32)
+            if b == 0:
+                nc.vector.tensor_copy(out=dst, in_=src)
+            else:
+                nc.scalar.copy(out=dst, in_=src)
 
         xw = x_sb[:].bitcast(F32)
         xt_of = {}
@@ -132,17 +135,14 @@ def tile_conv2dlinalgrmsnorm_t_kernel(tc, hidden_states, conv_w, norm_w, out):
         y_of = {}
         stat_of = {}
 
-        def transposes(k):
-            banks = []
-            for b in range(2):
-                xt = psum_x.tile([P, 2, 2, P], F32, tag="xt")
-                for a in range(2):
-                    t = RT * k + 2 * b + a
-                    for u in range(2):
-                        c0 = 256 * t + P * u
-                        nc.tensor.transpose(xt[:, a, u, :], xw[:, c0 : c0 + P], ident[:])
-                banks.append(xt)
-            xt_of[k] = banks
+        def transposes(k, b):
+            xt = psum_x.tile([P, 2, 2, P], F32, tag="xt")
+            for a in range(2):
+                t = RT * k + 2 * b + a
+                for u in range(2):
+                    c0 = 256 * t + P * u
+                    nc.tensor.transpose(xt[:, a, u, :], xw[:, c0 : c0 + P], ident[:])
+            xt_of[(k, b)] = xt
 
         def copy_out(k, b, on_vector):
             if b == 0:
@@ -150,7 +150,7 @@ def tile_conv2dlinalgrmsnorm_t_kernel(tc, hidden_states, conv_w, norm_w, out):
                 grp_of[k] = grp
             g32 = grp_of[k][:].bitcast(F32)
             dst = g32[:, 512 * b : 512 * b + 512].rearrange("p (a r u) -> p a r u", a=2, r=P, u=2)
-            src = xt_of[k][b][:].rearrange("p a u r -> p a r u")
+            src = xt_of[(k, b)][:].rearrange("p a u r -> p a r u")
             if on_vector:
                 nc.vector.tensor_copy(out=dst, in_=src)
             else:
@@ -167,7 +167,7 @@ def tile_conv2dlinalgrmsnorm_t_kernel(tc, hidden_states, conv_w, norm_w, out):
             banks = []
             for b in range(2):
                 y = psum_y.tile([P, 2, K], F32, tag="y")
-                if b < DUMMIES:
+                if k > 0 and b < DUMMIES:
                     nc.tensor.matmul_mx(
                         out=y[:].rearrange("p a k -> p (a k)"),
                         lhsT=xc[:, 0:P].bitcast(FP8X4),
@@ -193,32 +193,32 @@ def tile_conv2dlinalgrmsnorm_t_kernel(tc, hidden_states, conv_w, norm_w, out):
 
         def squares(k):
             q = stage.tile([P, RT], F32, tag="q")
-            for j in range(RT):
-                nc.scalar.activation(
-                    out=junk[:],
-                    in_=y_of[k][j // 2][:, j % 2, :],
-                    func=ACT.Square,
-                    accum_out=q[:, j : j + 1],
-                )
-            stat_of[k] = q
-
-        def reciprocal(k):
             n = stage.tile([P, RT], F32, tag="n")
+            for j0, j1 in cuts(k):
+                for j in range(j0, j1):
+                    nc.scalar.activation(
+                        out=junk[:],
+                        in_=y_of[k][j // 2][:, j % 2, :],
+                        func=ACT.Square,
+                        accum_out=q[:, j : j + 1],
+                    )
+                nc.scalar.activation(
+                    out=n[:, j0:j1],
+                    in_=q[:, j0:j1],
+                    func=ACT.Sqrt,
+                    bias=epsb[:],
+                    scale=1.0 / (LAYERS * LAYERS),
+                )
             r = stage.tile([P, RT], F32, tag="r")
-            nc.gpsimd.tensor_scalar(
-                out=n[:],
-                in0=stat_of[k][:],
-                scalar1=1.0 / (LAYERS * LAYERS),
-                scalar2=EPS * H,
-                op0=ALU.mult,
-                op1=ALU.add,
-            )
-            nc.gpsimd.tensor_tensor(out=r[:], in0=n[:], in1=mhalf[:], op=ALU.pow)
-            stat_of[k] = r
+            stat_of[k] = (n, r)
 
-        def final(k):
-            r = stat_of[k]
-            for j in range(RT):
+        def reciprocal(k, j0, j1):
+            n, r = stat_of[k]
+            nc.vector.reciprocal(out=r[:, j0:j1], in_=n[:, j0:j1])
+
+        def final(k, j0, j1):
+            r = stat_of[k][1]
+            for j in range(j0, j1):
                 t = RT * k + j
                 nc.vector.scalar_tensor_tensor(
                     out=out_sb[:, t * K : (t + 1) * K],
@@ -228,8 +228,19 @@ def tile_conv2dlinalgrmsnorm_t_kernel(tc, hidden_states, conv_w, norm_w, out):
                     op0=ALU.mult,
                     op1=ALU.mult,
                 )
-            c0 = RT * k * K
-            nc.sync.dma_start(out=ov[:, c0 : c0 + RT * K], in_=out_sb[:, c0 : c0 + RT * K])
+
+        def store(k, j0, j1):
+            c0 = (RT * k + j0) * K
+            c1 = (RT * k + j1) * K
+            nc.sync.dma_start(out=ov[:, c0:c1], in_=out_sb[:, c0:c1])
+
+        def cuts(k):
+            if k == ROUNDS - 1:
+                return [(0, 2), (2, 4)]
+            return [(0, RT)]
+
+        def on_vector(k, b):
+            return b == 1 or k % 2 == 0
 
         w_sum(0)
         nw_ps = psum_x.tile([P, K], F32, tag="xt")
@@ -248,40 +259,42 @@ def tile_conv2dlinalgrmsnorm_t_kernel(tc, hidden_states, conv_w, norm_w, out):
         w_sum(6)
         w_sum(7)
         w_round(1)
-        transposes(0)
+        transposes(0, 0)
         w_back(1)
-        copy_out(0, 0, True)
-        copy_out(0, 1, True)
+        copy_out(0, 0, False)
         w_back_copy(1)
-        transposes(1)
+        transposes(0, 1)
         w_forth(1)
-        copy_out(1, 0, False)
-        copy_out(1, 1, False)
-        w_forth_copy(1)
+        copy_out(0, 1, True)
         quantise(0)
+        w_forth_copy(1)
         nc.vector.quantize_mx(out=w_codes[:].bitcast(FP8X4), scales=w_scales[:], in_=wg[:])
-        for r in range(2, LEAD + 1):
-            transposes(r)
-            copy_out(r, 0, False)
-            copy_out(r, 1, False)
-            quantise(r - 1)
-        transposes(LEAD + 1)
+        transposes(1, 0)
+        transposes(1, 1)
+        copy_out(1, 0, False)
+        copy_out(1, 1, True)
         passes(0)
 
         for k in range(ROUNDS + 1):
-            a = k + LEAD + 1
+            a = k + 2
             if a < ROUNDS:
-                copy_out(a, 0, False)
-                copy_out(a, 1, a % 4 != 0)
-            if a + 1 < ROUNDS:
-                transposes(a + 1)
-            if a - 1 < ROUNDS:
-                quantise(a - 1)
-            if k >= 1:
-                reciprocal(k - 1)
+                transposes(a, 0)
+                transposes(a, 1)
+            if 1 <= k < ROUNDS:
+                reciprocal(k - 1, 0, RT)
+                final(k - 1, 0, 1)
+            if k + 1 < ROUNDS:
+                quantise(k + 1)
+                passes(k + 1)
+            if 1 <= k < ROUNDS:
+                final(k - 1, 1, RT)
+                store(k - 1, 0, RT)
             if k < ROUNDS:
                 squares(k)
-            if k >= 1:
-                final(k - 1)
-            if k + 1 < ROUNDS:
-                passes(k + 1)
+            if a < ROUNDS:
+                copy_out(a, 0, on_vector(a, 0))
+                copy_out(a, 1, on_vector(a, 1))
+        for j0, j1 in cuts(ROUNDS - 1):
+            reciprocal(ROUNDS - 1, j0, j1)
+            final(ROUNDS - 1, j0, j1)
+            store(ROUNDS - 1, j0, j1)

@@ -236,11 +236,11 @@ def tile_conv2dlinalgrmsnorm_t_kernel(tc, hidden_states, conv_w, norm_w, out):
 
         def cuts(k):
             if k == ROUNDS - 1:
-                return [(0, 2), (2, 4)]
+                return [(0, 2), (2, 3), (3, 4)]
             return [(0, RT)]
 
         def on_vector(k, b):
-            return b == 1 or k % 2 == 0
+            return b == 1
 
         w_sum(0)
         nw_ps = psum_x.tile([P, K], F32, tag="xt")

import math
from contextlib import ExitStack

import concourse.mybir as mybir
from concourse.masks import make_identity

F32 = mybir.dt.float32
BF16 = mybir.dt.bfloat16
U32 = mybir.dt.uint32
U8 = mybir.dt.uint8
FP8X4 = mybir.dt.float8_e4m3fn_x4
ALU = mybir.AluOpType
ACT = mybir.ActivationFunctionType

P = 128
TOKENS = 8192
H = 512
K = 256
LAYERS = 20
EPS = 1e-06
TILES = TOKENS // P
RT = 4
ROUNDS = TILES // RT
DUMMIES = 2

FLOPS = 2 * TOKENS * H * K

W_CHUNKS = [(0, 1), (1, 2), (2, 4), (4, 6), (6, 7), (7, 8)]
X_CHUNKS = [(0, 4), (4, 8), (8, 12), (12, 16), (16, 24), (24, 32), (32, 40), (40, 48), (48, 56), (56, 64)]


def tile_conv2dlinalgrmsnorm_t_kernel(tc, hidden_states, conv_w, norm_w, out):
    nc = tc.nc
    xv = hidden_states.flatten_outer_dims().rearrange("(p t) h -> p (t h)", t=TILES)
    ov = out.flatten_outer_dims().rearrange("(p t) k -> p (t k)", t=TILES)
    wv = conv_w.flatten_outer_dims().rearrange("(i p g) h -> p i g h", i=5, p=P, g=8)

    with ExitStack() as ctx:
        keep = ctx.enter_context(tc.tile_pool(name="keep", bufs=1))
        stage = ctx.enter_context(tc.tile_pool(name="stage", bufs=3))
        codes = ctx.enter_context(tc.tile_pool(name="codes", bufs=3))
        psum_x = ctx.enter_context(tc.psum_pool(name="psum_x", bufs=3))
        psum_y = ctx.enter_context(tc.psum_pool(name="psum_y", bufs=5))
        ctx.enter_context(tc.manual_schedule())

        w5 = keep.tile([P, 5, 8, H], BF16)
        x_sb = keep.tile([P, TILES * H], BF16)
        out_sb = keep.tile([P, TILES * K], F32)
        ident = keep.tile([P, P], F32)
        ident_b = keep.tile([P, P], BF16)
        sel_f = keep.tile([P, 32], F32)
        sel = keep.tile([P, 32], BF16)
        ones = keep.tile([P, P], BF16)
        nwz = keep.tile([P, K], BF16)
        nwp = keep.tile([P, K], F32)
        epsb = keep.tile([P, 1], F32)
        warm = keep.tile([P, 1], F32)
        junk = keep.tile([P, K], BF16)
        ws1 = keep.tile([P, 2, 4, P], BF16)
        ws3 = keep.tile([P, 2, H], BF16)
        wg = keep.tile([P, 4 * K], BF16, align_bytes=64)
        w_codes = keep.tile([P, K], U32, align_bytes=64)
        w_scales = keep.tile([P, K], U8, align_bytes=64)

        nc.vector.memset(nwz[:], 0.0)
        nc.vector.memset(epsb[:], EPS * H)
        nc.vector.memset(ones[:], 1.0)
        first = True
        for g0, g1 in W_CHUNKS:
            nc.sync.dma_start(out=w5[:, :, g0:g1, :], in_=wv[:, :, g0:g1, :])
            if first:
                nc.sync.dma_start(out=nwz[0:1, :], in_=norm_w.unsqueeze(0))
                first = False
        for t0, t1 in X_CHUNKS:
            nc.sync.dma_start(out=x_sb[:, t0 * H : t1 * H], in_=xv[:, t0 * H : t1 * H])
        nc.scalar.activation(out=warm[:], in_=epsb[:], func=ACT.Sqrt)
        make_identity(nc, ident[:])
        nc.vector.tensor_reduce(
            out=sel_f[:],
            in_=ident[:].rearrange("p (a n) -> p n a", a=4),
            axis=mybir.AxisListType.X,
            op=ALU.add,
        )
        nc.vector.tensor_copy(out=sel[:], in_=sel_f[:])
        nc.vector.tensor_copy(out=ident_b[:], in_=ident[:])

        wt0 = psum_y.tile([P, 4, P], F32, tag="y")
        wt1 = psum_y.tile([P, 4, P], F32, tag="y")
        wt = [wt0, wt1]
        s2 = psum_y.tile([P, 2, H], BF16, tag="y")
        s4 = psum_y.tile([P, 4, 2, P], BF16, tag="y")
        wg4 = wg[:].rearrange("p (j g t) -> p j g t", j=32, g=8, t=4)

        def w_sum(g):
            b, gl = divmod(g, 4)
            for t in range(4):
                for i in range(5):
                    nc.tensor.matmul(
                        out=wt[b][:, t, 32 * gl : 32 * gl + 32],
                        lhsT=w5[:, i, g, P * t : P * t + P],
                        rhs=sel[:],
                        start=(i == 0),
                        stop=(i == 4),
                    )

        def w_round(b):
            nc.vector.tensor_copy(out=ws1[:, b, :, :], in_=wt[b][:])

        def w_back(b):
            for t in range(4):
                nc.tensor.transpose(s2[:, b, P * t : P * t + P], ws1[:, b, t, :], ident_b[:])

        def w_back_copy(b):
            nc.scalar.copy(out=ws3[:, b, :], in_=s2[:, b, :])

        def w_forth(b):
            for t in range(4):
                u, e = divmod(t, 2)
                nc.tensor.transpose(
                    s4[:, t, b, :], ws3[:, b, 256 * u + e : 256 * u + 256 : 2], ident_b[:]
                )

        def w_forth_copy(b):
            dst = wg4[:, :, 4 * b : 4 * b + 4, :]
            src = s4[:, :, b, :].rearrange("p t (g j) -> p j g t", g=4, j=32)
            if b == 0:
                nc.vector.tensor_copy(out=dst, in_=src)
            else:
                nc.scalar.copy(out=dst, in_=src)

        xw = x_sb[:].bitcast(F32)
        xt_of = {}
        grp_of = {}
        code_of = {}
        y_of = {}
        stat_of = {}

        def transposes(k, b):
            xt = psum_x.tile([P, 2, 2, P], F32, tag="xt")
            for a in range(2):
                t = RT * k + 2 * b + a
                for u in range(2):
                    c0 = 256 * t + P * u
                    nc.tensor.transpose(xt[:, a, u, :], xw[:, c0 : c0 + P], ident[:])
            xt_of[(k, b)] = xt

        def copy_out(k, b, on_vector):
            if b == 0:
                grp = stage.tile([P, RT * H], BF16, align_bytes=64, tag="grp")
                grp_of[k] = grp
            g32 = grp_of[k][:].bitcast(F32)
            dst = g32[:, 512 * b : 512 * b + 512].rearrange("p (a r u) -> p a r u", a=2, r=P, u=2)
            src = xt_of[(k, b)][:].rearrange("p a u r -> p a r u")
            if on_vector:
                nc.vector.tensor_copy(out=dst, in_=src)
            else:
                nc.scalar.copy(out=dst, in_=src)

        def quantise(k):
            xc = codes.tile([P, RT * P], U32, align_bytes=64, tag="xc")
            xs = codes.tile([P, RT * P], U8, align_bytes=64, tag="xs")
            nc.vector.quantize_mx(out=xc[:].bitcast(FP8X4), scales=xs[:], in_=grp_of[k][:])
            code_of[k] = (xc, xs)

        def passes(k):
            xc, xs = code_of[k]
            banks = []
            for b in range(2):
                y = psum_y.tile([P, 2, K], F32, tag="y")
                if k > 0 and b < DUMMIES:
                    nc.tensor.matmul_mx(
                        out=y[:].rearrange("p a k -> p (a k)"),
                        lhsT=xc[:, 0:P].bitcast(FP8X4),
                        lhsT_scale=xs[:, 0:P],
                        rhs=xc[:].bitcast(FP8X4),
                        rhs_scale=xs[:],
                        start=True,
                        stop=True,
                    )
                for a in range(2):
                    c0 = P * (2 * b + a)
                    nc.tensor.matmul_mx(
                        out=y[:, a, :],
                        lhsT=xc[:, c0 : c0 + P].bitcast(FP8X4),
                        lhsT_scale=xs[:, c0 : c0 + P],
                        rhs=w_codes[:].bitcast(FP8X4),
                        rhs_scale=w_scales[:],
                        start=True,
                        stop=True,
                    )
                banks.append(y)
            y_of[k] = banks

        def squares(k):
            q = stage.tile([P, RT], F32, tag="q")
            n = stage.tile([P, RT], F32, tag="n")
            for j0, j1 in cuts(k):
                for j in range(j0, j1):
                    nc.scalar.activation(
                        out=junk[:],
                        in_=y_of[k][j // 2][:, j % 2, :],
                        func=ACT.Square,
                        accum_out=q[:, j : j + 1],
                    )
                nc.scalar.activation(
                    out=n[:, j0:j1],
                    in_=q[:, j0:j1],
                    func=ACT.Sqrt,
                    bias=epsb[:],
                    scale=1.0 / (LAYERS * LAYERS),
                )
            r = stage.tile([P, RT], F32, tag="r")
            stat_of[k] = (n, r)

        def reciprocal(k, j0, j1):
            n, r = stat_of[k]
            nc.vector.reciprocal(out=r[:, j0:j1], in_=n[:, j0:j1])

        def final(k, j0, j1):
            r = stat_of[k][1]
            for j in range(j0, j1):
                t = RT * k + j
                nc.vector.scalar_tensor_tensor(
                    out=out_sb[:, t * K : (t + 1) * K],
                    in0=y_of[k][j // 2][:, j % 2, :],
                    scalar=r[:, j : j + 1],
                    in1=nwp[:],
                    op0=ALU.mult,
                    op1=ALU.mult,
                )

        def store(k, j0, j1):
            c0 = (RT * k + j0) * K
            c1 = (RT * k + j1) * K
            nc.sync.dma_start(out=ov[:, c0:c1], in_=out_sb[:, c0:c1])

        def cuts(k):
            if k == ROUNDS - 1:
                return [(0, 2), (2, 3), (3, 4)]
            return [(0, RT)]

        def on_vector(k, b):
            return b == 1

        w_sum(0)
        nw_ps = psum_x.tile([P, K], F32, tag="xt")
        nc.tensor.matmul(out=nw_ps[:], lhsT=ones[:], rhs=nwz[:], start=True, stop=True)
        nc.vector.tensor_scalar_mul(out=nwp[:], in0=nw_ps[:], scalar1=math.sqrt(H) / LAYERS)
        w_sum(1)
        w_sum(2)
        w_sum(3)
        w_round(0)
        w_sum(4)
        w_back(0)
        w_back_copy(0)
        w_sum(5)
        w_forth(0)
        w_forth_copy(0)
        w_sum(6)
        w_sum(7)
        w_round(1)
        transposes(0, 0)
        w_back(1)
        copy_out(0, 0, False)
        w_back_copy(1)
        transposes(0, 1)
        w_forth(1)
        copy_out(0, 1, True)
        quantise(0)
        w_forth_copy(1)
        nc.vector.quantize_mx(out=w_codes[:].bitcast(FP8X4), scales=w_scales[:], in_=wg[:])
        transposes(1, 0)
        transposes(1, 1)
        copy_out(1, 0, False)
        copy_out(1, 1, True)
        passes(0)

        for k in range(ROUNDS + 1):
            a = k + 2
            if a < ROUNDS:
                transposes(a, 0)
                transposes(a, 1)
            if 1 <= k < ROUNDS:
                reciprocal(k - 1, 0, RT)
                final(k - 1, 0, 1)
            if k + 1 < ROUNDS:
                quantise(k + 1)
                passes(k + 1)
            if 1 <= k < ROUNDS:
                final(k - 1, 1, RT)
                store(k - 1, 0, RT)
            if k < ROUNDS:
                squares(k)
            if a < ROUNDS:
                copy_out(a, 0, on_vector(a, 0))
                copy_out(a, 1, on_vector(a, 1))
        for j0, j1 in cuts(ROUNDS - 1):
            reciprocal(ROUNDS - 1, j0, j1)
            final(ROUNDS - 1, j0, j1)
            store(ROUNDS - 1, j0, j1)
